import numpy as np
import ml_dtypes


def mxq(x, axis, fmt="e4m3"):
    dtype, down = {"e4m3": (ml_dtypes.float8_e4m3fn, 7), "e5m2": (ml_dtypes.float8_e5m2, 14)}[fmt]
    v = np.moveaxis(np.asarray(x, np.float32).astype(ml_dtypes.bfloat16).astype(np.float64), axis, -1)
    blocks = v.reshape(v.shape[:-1] + (-1, 32))
    amax = np.abs(blocks).max(-1, keepdims=True)
    byte = np.maximum(np.where(amax > 0, np.frexp(amax)[1] - 1 + 127, 0) - down, 1)
    scale = np.exp2(byte - 127.0)
    codes = (blocks / scale).astype(np.float32).astype(dtype).astype(np.float64)
    return np.moveaxis((codes * scale).reshape(v.shape), -1, axis)


WIDE = False


def mx_kscale(k):
    if not WIDE:
        return np.ones(k)
    levels = np.array([10, -10, 5, -5, 0])
    a = np.random.permutation(np.resize(levels, k // 512 * 4)).reshape(k // 512, 4)
    idx = np.arange(k)
    return np.exp2(a[idx // 512, idx % 128 // 32])


BF16 = ml_dtypes.bfloat16


def bf(x):
    return np.asarray(x, np.float32).astype(BF16)


def f64(x):
    return np.asarray(x).astype(np.float64)


B, H, SQ, SK, DK = 1, 4, 1024, 512, 512
D = H * DK


def setup_inputs():
    s = mx_kscale(D)
    g = np.random.standard_normal
    return {"q": bf(g((B, H, SQ, DK)) * 1.4),
            "k": bf(g((B, H, SK, DK)) * 1.4),
            "image_feat": bf(g((B, SK, D)) * 0.13 * np.sqrt(SK) * s),
            "W3": bf(g((D, D)) * 2.0 / np.sqrt(D) / s[None, :]),
            "b3": bf(g(D) * 0.4)}


def reference(q, k, image_feat, W3, b3):
    imf = (mxq(f64(image_feat), 2, "e4m3") @ mxq(f64(W3), 1, "e4m3").T) + f64(b3)
    imf = imf.reshape(B, SK, H, DK).transpose(0, 2, 1, 3)
    s = f64(q) @ f64(k).transpose(0, 1, 3, 2) / np.sqrt(DK)
    e = np.exp(s - s.max(-1, keepdims=True))
    return (mxq(e, 3, "e4m3") @ mxq(imf, 2, "e4m3")) / e.sum(-1, keepdims=True)

@@ -1,0 +1,325 @@
+import math
+from contextlib import ExitStack
+
+import concourse.bass as bass
+import concourse.mybir as mybir
+import concourse.tile as tile
+from concourse.masks import make_identity
+
+F32 = mybir.dt.float32
+BF16 = mybir.dt.bfloat16
+U32 = mybir.dt.uint32
+U8 = mybir.dt.uint8
+FP8X4 = mybir.dt.float8_e4m3fn_x4
+ACT = mybir.ActivationFunctionType
+ALU = mybir.AluOpType
+AX = mybir.AxisListType
+
+P = 128
+H = 4
+SQ = 1024
+SK = 512
+DK = 512
+D = 2048
+NQT = H * SQ // P
+NOT = D // P
+NXT = SK // P
+NUNIT = NXT + NOT
+W_BUFS = 10
+SCALE = 1.0 / math.sqrt(DK)
+FLOPS = 2 * SK * D * D + 2 * (2 * H * SQ * SK * DK)
+
+MANUAL = True
+U_START = 1
+PV_PER_BUNCH = 2
+
+
+def tile_multiheadedattention_pa_kernel(tc, q, k, image_feat, W3, b3, out):
+    nc = tc.nc
+    with ExitStack() as ctx:
+        if MANUAL:
+            ctx.enter_context(tc.manual_schedule())
+        const = ctx.enter_context(tc.tile_pool(name="const", bufs=1))
+        raw = ctx.enter_context(tc.tile_pool(name="raw", bufs=1))
+        wraw = ctx.enter_context(tc.tile_pool(name="wraw", bufs=W_BUFS))
+        keep = ctx.enter_context(tc.tile_pool(name="keep", bufs=1))
+        grp = ctx.enter_context(tc.tile_pool(name="grp", bufs=3))
+        wq = ctx.enter_context(tc.tile_pool(name="wq", bufs=3))
+        tq = ctx.enter_context(tc.tile_pool(name="tq", bufs=3))
+        tk = ctx.enter_context(tc.tile_pool(name="tk", bufs=2))
+        ep = ctx.enter_context(tc.tile_pool(name="ep", bufs=3))
+        eq = ctx.enter_context(tc.tile_pool(name="eq", bufs=14))
+        small = ctx.enter_context(tc.tile_pool(name="small", bufs=3))
+        op = ctx.enter_context(tc.tile_pool(name="op", bufs=3))
+        ps_s = ctx.enter_context(tc.psum_pool(name="ps_s", bufs=2))
+        ps_t = ctx.enter_context(tc.psum_pool(name="ps_t", bufs=3))
+        ps_e = ctx.enter_context(tc.psum_pool(name="ps_e", bufs=1))
+        ps_a = ctx.enter_context(tc.psum_pool(name="ps_a", bufs=1))
+        ps_p = ctx.enter_context(tc.psum_pool(name="ps_p", bufs=1))
+
+        q_v = q[0].rearrange("h (p a) d -> h p (a d)", a=8)
+        k_v = k[0].rearrange("h (p t) d -> h p (t d)", t=4)
+        x_v = image_feat[0].rearrange("(p t) i -> t p i", t=4)
+        w_v = W3.rearrange("(a p) i -> a p i", p=P)
+        o_v = out[0].rearrange("h (p a) d -> h p a d", a=8)
+
+        ident_f = const.tile([P, P], F32)
+        make_identity(nc, ident_f[:])
+        ident_b = const.tile([P, P], BF16)
+        make_identity(nc, ident_b[:])
+        warm = const.tile([P, 1], F32)
+        nc.vector.memset(warm[:], 0.0)
+        warm2 = const.tile([P, 1], F32)
+        nc.scalar.activation(out=warm2[:], in_=warm[:], func=ACT.Exp)
+
+        k_raw = [raw.tile([P, 2048], BF16, name="k_raw%d" % h) for h in range(H)]
+        q_raw = [raw.tile([P, 4096], BF16, name="q_raw%d" % h) for h in range(H)]
+        x_raw = [raw.tile([P, 2048], BF16, name="x_raw%d" % t) for t in range(NXT)]
+        bias = const.tile([P, D], BF16)
+        w_raw = {}
+
+        def load_kq(h):
+            nc.sync.dma_start(out=k_raw[h][:], in_=k_v[h])
+            nc.sync.dma_start(out=q_raw[h][:, 0:2048], in_=q_v[h][:, 0:2048])
+            nc.sync.dma_start(out=q_raw[h][:, 2048:4096], in_=q_v[h][:, 2048:4096])
+
+        def load_w(ot):
+            w_t = wraw.tile([P, 2048], BF16, name="w_raw")
+            nc.sync.dma_start(out=w_t[:], in_=w_v[ot])
+            w_raw[ot] = w_t
+
+        load_kq(0)
+        for t in range(NXT):
+            nc.sync.dma_start(out=x_raw[t][:], in_=x_v[t])
+        for ot in range(0, 4):
+            load_w(ot)
+        nc.sync.dma_start(out=bias[:], in_=b3.partition_broadcast(P))
+        load_kq(1)
+        for ot in range(4, 8):
+            load_w(ot)
+        load_kq(2)
+        for ot in range(8, W_BUFS):
+            load_w(ot)
+        load_kq(3)
+
+        xc = keep.tile([P, NXT, 4, P], U32, align_bytes=64)
+        xs = keep.tile([P, NXT, 4, P], U8, align_bytes=64)
+        imf_c = [keep.tile([P, DK], U32, align_bytes=64, name="imf_c%d" % h) for h in range(H)]
+        imf_s = [keep.tile([P, DK], U8, align_bytes=64, name="imf_s%d" % h) for h in range(H)]
+
+        st = {}
+
+        def unit_raw(v):
+            return x_raw[v] if v < NXT else w_raw[v - NXT]
+
+        def u_job(v, gp):
+            box = {}
+
+            def tr(gl, u):
+                def go():
+                    if "b" not in box:
+                        box["b"] = ps_t.tile([P, 2, 2, P], F32, name="tw")
+                    c0 = P * (2 * (2 * gp + gl) + u)
+                    nc.tensor.transpose(box["b"][:, gl, u, :], unit_raw(v)[:].bitcast(F32)[:, c0:c0 + P], ident_f[:])
+                return go
+
+            def fin():
+                if gp == 0:
+                    st["g%d" % v] = grp.tile([P, 2048], BF16, align_bytes=64, name="grouped")
+                g_f = st["g%d" % v][:].bitcast(F32).rearrange("p (g c u) -> p g c u", g=4, u=2)
+                nc.scalar.copy(out=g_f[:, 2 * gp:2 * gp + 2, :, :], in_=box["b"][:].rearrange("p g u c -> p g c u"))
+                if gp == 1 and v >= NXT and v - NXT + W_BUFS < NOT:
+                    load_w(v - NXT + W_BUFS)
+            return [tr(gl, u) for gl in range(2) for u in range(2)], fin
+
+        def quant_u(v):
+            g_t = st["g%d" % v]
+            if v < NXT:
+                c_ap = xc[:, v, :, :].rearrange("p g c -> p (g c)")
+                s_ap = xs[:, v, :, :].rearrange("p g c -> p (g c)")
+            else:
+                wc = wq.tile([P, 4 * P], U32, align_bytes=64, name="wc")
+                ws = wq.tile([P, 4 * P], U8, align_bytes=64, name="ws")
+                st["wc%d" % (v - NXT)] = (wc, ws)
+                c_ap = wc[:]
+                s_ap = ws[:]
+            nc.vector.quantize_mx(out=c_ap.bitcast(FP8X4), scales=s_ap, in_=g_t[:])
+
+        def k_job(h, tp):
+            box = {}
+
+            def tr(u, tl):
+                def go():
+                    if "b" not in box:
+                        box["b"] = ps_t.tile([P, 2, 2, P], F32, name="tw")
+                    c0 = 256 * (2 * tp + tl) + P * u
+                    nc.tensor.transpose(box["b"][:, u, tl, :], k_raw[h][:].bitcast(F32)[:, c0:c0 + P], ident_f[:])
+                return go
+
+            def fin():
+                if tp == 0:
+                    st["kT%d" % h] = tk.tile([P, 1024], F32, name="kT")
+                dst = st["kT%d" % h][:].rearrange("p (u t c) -> p u t c", u=2, t=4)
+                nc.scalar.copy(out=dst[:, :, 2 * tp:2 * tp + 2, :], in_=box["b"][:])
+            return [tr(u, tl) for u in range(2) for tl in range(2)], fin
+
+        def q_job(m):
+            h, a0 = (2 * m) // 8, (2 * m) % 8
+            box = {}
+
+            def tr(al, u):
+                def go():
+                    if "b" not in box:
+                        box["b"] = ps_t.tile([P, 2, 2, P], F32, name="tw")
+                    c0 = 256 * (a0 + al) + P * u
+                    nc.tensor.transpose(box["b"][:, al, u, :], q_raw[h][:].bitcast(F32)[:, c0:c0 + P], ident_f[:])
+                return go
+
+            def fin():
+                st["qT%d" % m] = tq.tile([P, 512], F32, name="qT")
+                nc.scalar.copy(out=st["qT%d" % m][:], in_=box["b"][:].rearrange("p a u c -> p (a u c)"))
+            return [tr(al, u) for al in range(2) for u in range(2)], fin
+
+        def e_job(j):
+            box = {}
+
+            def tr(t):
+                def go():
+                    if "b" not in box:
+                        box["b"] = ps_e.tile([P, 4, P], BF16, name="et")
+                    nc.tensor.transpose(box["b"][:, t, :], st["e%d" % j][:, P * t:P * t + P], ident_b[:])
+                return go
+
+            def fin():
+                eg = ep.tile([P, P, 4], BF16, align_bytes=64, name="eg")
+                st["eg%d" % j] = eg
+                nc.vector.tensor_copy(out=eg[:], in_=box["b"][:].rearrange("p t c -> p c t"))
+            return [tr(t) for t in range(4)], fin
+
+        def quant_e(j):
+            eg = st["eg%d" % j]
+            ec = eq.tile([P, P], U32, align_bytes=64, name="ec")
+            es = eq.tile([P, P], U8, align_bytes=64, name="es")
+            st["ec%d" % j] = (ec, es)
+            nc.vector.quantize_mx(out=ec[:].bitcast(FP8X4), scales=es[:], in_=eg[:].rearrange("p c t -> p (c t)"))
+
+        def run_jobs(jobs):
+            for trs, fin in jobs:
+                for go in trs:
+                    go()
+                fin()
+
+        def qk_with_transposes(j, jobs):
+            flat = []
+            for trs, fin in jobs:
+                for n, go in enumerate(trs):
+                    flat.append((go, fin if n == len(trs) - 1 else None))
+            per = (len(flat) + 2) // 3
+            h, m, al = j // 8, j // 2, j % 2
+            s_t = ps_s.tile([P, SK], F32, name="s")
+            st["s%d" % j] = s_t
+            q_b = st["qT%d" % m][:].bitcast(BF16).rearrange("p (a u c e) -> p a u c e", a=2, u=2, e=2)
+            k_b = st["kT%d" % h][:].bitcast(BF16).rearrange("p (u c e) -> p u c e", u=2, e=2)
+            for n in range(4):
+                u, e = n // 2, n % 2
+                nc.tensor.matmul(s_t[:], lhsT=q_b[:, al, u, :, e], rhs=k_b[:, u, :, e], start=(n == 0), stop=(n == 3))
+                if n < 3:
+                    for go, fin in flat[per * n:per * (n + 1)]:
+                        go()
+                        if fin is not None:
+                            fin()
+
+        def softmax_max(j):
+            mx = small.tile([P, 1], F32, name="mx")
+            nc.vector.tensor_reduce(out=mx[:], in_=st["s%d" % j][:], axis=AX.X, op=ALU.max)
+            nb = small.tile([P, 1], F32, name="nb")
+            nc.vector.tensor_scalar(out=nb[:], in0=mx[:], scalar1=-SCALE, scalar2=None, op0=ALU.mult)
+            st["nb%d" % j] = nb
+
+        def softmax_exp(j):
+            e_t = ep.tile([P, SK], BF16, name="e")
+            rs = eq.tile([P, 1], F32, name="rs")
+            nc.scalar.activation(out=e_t[:], in_=st["s%d" % j][:], func=ACT.Exp, bias=st["nb%d" % j][:],
+                                 scale=SCALE, accum_out=rs[:])
+            st["e%d" % j] = e_t
+            st["rs%d" % j] = rs
+
+        def recip(j):
+            ri = eq.tile([P, 1], F32, name="ri")
+            nc.vector.reciprocal(out=ri[:], in_=st["rs%d" % j][:])
+            st["ri%d" % j] = ri
+
+        def stage1(ot):
+            wc, ws = st["wc%d" % ot]
+            acc = ps_a.tile([P, 4, P], F32, name="acc")
+            for t in range(NXT):
+                for g in range(4):
+                    nc.tensor.matmul_mx(out=acc[:, t, :], lhsT=xc[:, t, g, :].bitcast(FP8X4), lhsT_scale=xs[:, t, g, :],
+                                        rhs=wc[:, P * g:P * g + P].bitcast(FP8X4), rhs_scale=ws[:, P * g:P * g + P],
+                                        start=(g == 0), stop=(g == 3))
+            ig = grp.tile([P, P, 4], BF16, align_bytes=64, name="ig")
+            nc.vector.tensor_tensor(out=ig[:], in0=acc[:].rearrange("p t o -> p o t"),
+                                    in1=bias[:, P * ot:P * ot + P].unsqueeze(2).to_broadcast([P, P, 4]), op=ALU.add)
+            st["ig%d" % ot] = ig
+
+        def quant_imf(ot):
+            h, a = ot // 4, ot % 4
+            nc.vector.quantize_mx(out=imf_c[h][:, P * a:P * a + P].bitcast(FP8X4), scales=imf_s[h][:, P * a:P * a + P],
+                                  in_=st["ig%d" % ot][:].rearrange("p o t -> p (o t)"))
+
+        def pv(j):
+            h, a = j // 8, j % 8
+            ec, es = st["ec%d" % j]
+            pv_t = ps_p.tile([P, DK], F32, name="pv")
+            nc.tensor.matmul_mx(out=pv_t[:], lhsT=ec[:].bitcast(FP8X4), lhsT_scale=es[:], rhs=imf_c[h][:].bitcast(FP8X4),
+                                rhs_scale=imf_s[h][:], start=True, stop=True)
+            if a % 2 == 0:
+                st["o"] = op.tile([P, 2, DK], F32, name="o_sb")
+            nc.scalar.activation(out=st["o"][:, a % 2, :], in_=pv_t[:], func=ACT.Copy, scale=st["ri%d" % j][:])
+            if a % 2 == 1:
+                nc.sync.dma_start(out=o_v[h][:, a - 1:a + 1, :], in_=st["o"][:])
+
+        run_jobs([k_job(0, 0), k_job(0, 1), q_job(0)])
+        next_pv = 0
+        i = 0
+        while next_pv < NQT:
+            jobs = []
+            v = i - U_START
+            if 0 <= v < NUNIT:
+                jobs.append(u_job(v, 0))
+            if 1 <= i <= NQT:
+                jobs.append(e_job(i - 1))
+            if 0 <= v < NUNIT:
+                jobs.append(u_job(v, 1))
+            if i % 2 == 0 and i // 2 + 1 < NQT // 2:
+                jobs.append(q_job(i // 2 + 1))
+            if i % 8 in (3, 5) and i // 8 + 1 < H:
+                jobs.append(k_job(i // 8 + 1, (i % 8) // 4))
+            if i < NQT:
+                qk_with_transposes(i, jobs)
+            else:
+                run_jobs(jobs)
+            ot_done = i - U_START - NXT - 2
+            if 0 <= ot_done < NOT:
+                quant_imf(ot_done)
+            if 1 <= i <= NQT:
+                quant_e(i - 1)
+                recip(i - 1)
+            if i < NQT:
+                softmax_max(i)
+            if 0 <= v < NUNIT:
+                quant_u(v)
+            todo = []
+            while len(todo) < PV_PER_BUNCH and next_pv < NQT and next_pv <= i - 1 and i >= U_START + NXT + 4 * (next_pv // 8) + 3 + 2:
+                todo.append(next_pv)
+                next_pv += 1
+            if todo:
+                pv(todo[0])
+            if i < NQT:
+                softmax_exp(i)
+            ot = i - U_START - NXT - 1
+            if 0 <= ot < NOT:
+                stage1(ot)
+            for j in todo[1:]:
+                pv(j)
+            i += 1

@@ -32,6 +32,13 @@ FLOPS = 2 * SK * D * D + 2 * (2 * H * SQ * SK * DK)
 MANUAL = True
 U_START = 1
 PV_PER_BUNCH = 2
+E_LAG = 2
+PV_LAG = 1
+K_AT = (5, 7)
+K_ON_V = True
+Q_ON_V = 0
+U_ON_V = 0
+S1_LAG = 1
 
 
 def tile_multiheadedattention_pa_kernel(tc, q, k, image_feat, W3, b3, out):
@@ -44,10 +51,10 @@ def tile_multiheadedattention_pa_kernel(tc, q, k, image_feat, W3, b3, out):
         wraw = ctx.enter_context(tc.tile_pool(name="wraw", bufs=W_BUFS))
         keep = ctx.enter_context(tc.tile_pool(name="keep", bufs=1))
         grp = ctx.enter_context(tc.tile_pool(name="grp", bufs=3))
-        wq = ctx.enter_context(tc.tile_pool(name="wq", bufs=3))
+        wq = ctx.enter_context(tc.tile_pool(name="wq", bufs=S1_LAG + 2))
         tq = ctx.enter_context(tc.tile_pool(name="tq", bufs=3))
         tk = ctx.enter_context(tc.tile_pool(name="tk", bufs=2))
-        ep = ctx.enter_context(tc.tile_pool(name="ep", bufs=3))
+        ep = ctx.enter_context(tc.tile_pool(name="ep", bufs=E_LAG + 2))
         eq = ctx.enter_context(tc.tile_pool(name="eq", bufs=14))
         small = ctx.enter_context(tc.tile_pool(name="small", bufs=3))
         op = ctx.enter_context(tc.tile_pool(name="op", bufs=3))
@@ -81,6 +88,8 @@ def tile_multiheadedattention_pa_kernel(tc, q, k, image_feat, W3, b3, out):
         def load_kq(h):
             nc.sync.dma_start(out=k_raw[h][:], in_=k_v[h])
             nc.sync.dma_start(out=q_raw[h][:, 0:2048], in_=q_v[h][:, 0:2048])
+
+        def load_q2(h):
             nc.sync.dma_start(out=q_raw[h][:, 2048:4096], in_=q_v[h][:, 2048:4096])
 
         def load_w(ot):
@@ -89,18 +98,24 @@ def tile_multiheadedattention_pa_kernel(tc, q, k, image_feat, W3, b3, out):
             w_raw[ot] = w_t
 
         load_kq(0)
+        load_q2(0)
         for t in range(NXT):
             nc.sync.dma_start(out=x_raw[t][:], in_=x_v[t])
-        for ot in range(0, 4):
+        for ot in range(0, 2):
+            load_w(ot)
+        load_kq(1)
+        for ot in range(2, 4):
             load_w(ot)
         nc.sync.dma_start(out=bias[:], in_=b3.partition_broadcast(P))
-        load_kq(1)
+        load_q2(1)
         for ot in range(4, 8):
             load_w(ot)
         load_kq(2)
+        load_q2(2)
         for ot in range(8, W_BUFS):
             load_w(ot)
         load_kq(3)
+        load_q2(3)
 
         xc = keep.tile([P, NXT, 4, P], U32, align_bytes=64)
         xs = keep.tile([P, NXT, 4, P], U8, align_bytes=64)
@@ -127,7 +142,10 @@ def tile_multiheadedattention_pa_kernel(tc, q, k, image_feat, W3, b3, out):
                 if gp == 0:
                     st["g%d" % v] = grp.tile([P, 2048], BF16, align_bytes=64, name="grouped")
                 g_f = st["g%d" % v][:].bitcast(F32).rearrange("p (g c u) -> p g c u", g=4, u=2)
-                nc.scalar.copy(out=g_f[:, 2 * gp:2 * gp + 2, :, :], in_=box["b"][:].rearrange("p g u c -> p g c u"))
+                if U_ON_V and gp == 0 and v % U_ON_V == 0:
+                    nc.vector.tensor_copy(out=g_f[:, 2 * gp:2 * gp + 2, :, :], in_=box["b"][:].rearrange("p g u c -> p g c u"))
+                else:
+                    nc.scalar.copy(out=g_f[:, 2 * gp:2 * gp + 2, :, :], in_=box["b"][:].rearrange("p g u c -> p g c u"))
                 if gp == 1 and v >= NXT and v - NXT + W_BUFS < NOT:
                     load_w(v - NXT + W_BUFS)
             return [tr(gl, u) for gl in range(2) for u in range(2)], fin
@@ -160,7 +178,10 @@ def tile_multiheadedattention_pa_kernel(tc, q, k, image_feat, W3, b3, out):
                 if tp == 0:
                     st["kT%d" % h] = tk.tile([P, 1024], F32, name="kT")
                 dst = st["kT%d" % h][:].rearrange("p (u t c) -> p u t c", u=2, t=4)
-                nc.scalar.copy(out=dst[:, :, 2 * tp:2 * tp + 2, :], in_=box["b"][:])
+                if K_ON_V:
+                    nc.vector.tensor_copy(out=dst[:, :, 2 * tp:2 * tp + 2, :], in_=box["b"][:])
+                else:
+                    nc.scalar.copy(out=dst[:, :, 2 * tp:2 * tp + 2, :], in_=box["b"][:])
             return [tr(u, tl) for u in range(2) for tl in range(2)], fin
 
         def q_job(m):
@@ -177,7 +198,10 @@ def tile_multiheadedattention_pa_kernel(tc, q, k, image_feat, W3, b3, out):
 
             def fin():
                 st["qT%d" % m] = tq.tile([P, 512], F32, name="qT")
-                nc.scalar.copy(out=st["qT%d" % m][:], in_=box["b"][:].rearrange("p a u c -> p (a u c)"))
+                if Q_ON_V and m % Q_ON_V == 0:
+                    nc.vector.tensor_copy(out=st["qT%d" % m][:], in_=box["b"][:].rearrange("p a u c -> p (a u c)"))
+                else:
+                    nc.scalar.copy(out=st["qT%d" % m][:], in_=box["b"][:].rearrange("p a u c -> p (a u c)"))
             return [tr(al, u) for al in range(2) for u in range(2)], fin
 
         def e_job(j):
@@ -287,37 +311,37 @@ def tile_multiheadedattention_pa_kernel(tc, q, k, image_feat, W3, b3, out):
             v = i - U_START
             if 0 <= v < NUNIT:
                 jobs.append(u_job(v, 0))
-            if 1 <= i <= NQT:
-                jobs.append(e_job(i - 1))
+            if 0 <= i - E_LAG < NQT:
+                jobs.append(e_job(i - E_LAG))
             if 0 <= v < NUNIT:
                 jobs.append(u_job(v, 1))
             if i % 2 == 0 and i // 2 + 1 < NQT // 2:
                 jobs.append(q_job(i // 2 + 1))
-            if i % 8 in (3, 5) and i // 8 + 1 < H:
-                jobs.append(k_job(i // 8 + 1, (i % 8) // 4))
+            if i % 8 in K_AT and i // 8 + 1 < H:
+                jobs.append(k_job(i // 8 + 1, K_AT.index(i % 8)))
             if i < NQT:
                 qk_with_transposes(i, jobs)
             else:
                 run_jobs(jobs)
-            ot_done = i - U_START - NXT - 2
+            ot_done = i - U_START - NXT - S1_LAG - 1
             if 0 <= ot_done < NOT:
                 quant_imf(ot_done)
-            if 1 <= i <= NQT:
-                quant_e(i - 1)
-                recip(i - 1)
+            if 0 <= i - E_LAG < NQT:
+                quant_e(i - E_LAG)
+                recip(i - E_LAG)
             if i < NQT:
                 softmax_max(i)
             if 0 <= v < NUNIT:
                 quant_u(v)
             todo = []
-            while len(todo) < PV_PER_BUNCH and next_pv < NQT and next_pv <= i - 1 and i >= U_START + NXT + 4 * (next_pv // 8) + 3 + 2:
+            while len(todo) < PV_PER_BUNCH and next_pv < NQT and next_pv <= i - E_LAG - PV_LAG and i >= U_START + NXT + 4 * (next_pv // 8) + 3 + S1_LAG + 1:
                 todo.append(next_pv)
                 next_pv += 1
             if todo:
                 pv(todo[0])
             if i < NQT:
                 softmax_exp(i)
-            ot = i - U_START - NXT - 1
+            ot = i - U_START - NXT - S1_LAG
             if 0 <= ot < NOT:
                 stage1(ot)
             for j in todo[1:]:

@@ -32,8 +32,12 @@ FLOPS = 2 * SK * D * D + 2 * (2 * H * SQ * SK * DK)
 MANUAL = True
 U_START = 1
 PV_PER_BUNCH = 2
+GAP_SPLIT = (0, 1, 0)
 E_LAG = 2
 PV_LAG = 1
+O_BUFS = 6
+DRAIN_A = 2
+DRAIN_B = 2
 K_AT = (5, 7)
 K_ON_V = True
 Q_ON_V = 0
@@ -57,7 +61,7 @@ def tile_multiheadedattention_pa_kernel(tc, q, k, image_feat, W3, b3, out):
         ep = ctx.enter_context(tc.tile_pool(name="ep", bufs=E_LAG + 2))
         eq = ctx.enter_context(tc.tile_pool(name="eq", bufs=14))
         small = ctx.enter_context(tc.tile_pool(name="small", bufs=3))
-        op = ctx.enter_context(tc.tile_pool(name="op", bufs=3))
+        op = ctx.enter_context(tc.tile_pool(name="op", bufs=O_BUFS))
         ps_s = ctx.enter_context(tc.psum_pool(name="ps_s", bufs=2))
         ps_t = ctx.enter_context(tc.psum_pool(name="ps_t", bufs=3))
         ps_e = ctx.enter_context(tc.psum_pool(name="ps_e", bufs=1))
@@ -97,7 +101,10 @@ def tile_multiheadedattention_pa_kernel(tc, q, k, image_feat, W3, b3, out):
             nc.sync.dma_start(out=w_t[:], in_=w_v[ot])
             w_raw[ot] = w_t
 
-        load_kq(0)
+        nc.sync.dma_start(out=k_raw[0][:, 0:1024], in_=k_v[0][:, 0:1024])
+        nc.sync.dma_start(out=k_raw[0][:, 1024:2048], in_=k_v[0][:, 1024:2048])
+        nc.sync.dma_start(out=q_raw[0][:, 0:1024], in_=q_v[0][:, 0:1024])
+        nc.sync.dma_start(out=q_raw[0][:, 1024:2048], in_=q_v[0][:, 1024:2048])
         load_q2(0)
         for t in range(NXT):
             nc.sync.dma_start(out=x_raw[t][:], in_=x_v[t])
@@ -178,7 +185,7 @@ def tile_multiheadedattention_pa_kernel(tc, q, k, image_feat, W3, b3, out):
                 if tp == 0:
                     st["kT%d" % h] = tk.tile([P, 1024], F32, name="kT")
                 dst = st["kT%d" % h][:].rearrange("p (u t c) -> p u t c", u=2, t=4)
-                if K_ON_V:
+                if K_ON_V and not (h == 0 and tp == 1):
                     nc.vector.tensor_copy(out=dst[:, :, 2 * tp:2 * tp + 2, :], in_=box["b"][:])
                 else:
                     nc.scalar.copy(out=dst[:, :, 2 * tp:2 * tp + 2, :], in_=box["b"][:])
@@ -198,19 +205,20 @@ def tile_multiheadedattention_pa_kernel(tc, q, k, image_feat, W3, b3, out):
 
             def fin():
                 st["qT%d" % m] = tq.tile([P, 512], F32, name="qT")
-                if Q_ON_V and m % Q_ON_V == 0:
+                if m == 0 or (Q_ON_V and m % Q_ON_V == 0):
                     nc.vector.tensor_copy(out=st["qT%d" % m][:], in_=box["b"][:].rearrange("p a u c -> p (a u c)"))
                 else:
                     nc.scalar.copy(out=st["qT%d" % m][:], in_=box["b"][:].rearrange("p a u c -> p (a u c)"))
             return [tr(al, u) for al in range(2) for u in range(2)], fin
 
-        def e_job(j):
+        def e_job(j, pool=None, tag="et"):
+            pool = pool or ps_e
             box = {}
 
             def tr(t):
                 def go():
                     if "b" not in box:
-                        box["b"] = ps_e.tile([P, 4, P], BF16, name="et")
+                        box["b"] = pool.tile([P, 4, P], BF16, name=tag)
                     nc.tensor.transpose(box["b"][:, t, :], st["e%d" % j][:, P * t:P * t + P], ident_b[:])
                 return go
 
@@ -238,7 +246,9 @@ def tile_multiheadedattention_pa_kernel(tc, q, k, image_feat, W3, b3, out):
             for trs, fin in jobs:
                 for n, go in enumerate(trs):
                     flat.append((go, fin if n == len(trs) - 1 else None))
-            per = (len(flat) + 2) // 3
+            tot = sum(GAP_SPLIT)
+            ends = [(len(flat) * sum(GAP_SPLIT[:n + 1]) + tot - 1) // tot for n in range(3)]
+            begs = [0] + ends[:2]
             h, m, al = j // 8, j // 2, j % 2
             s_t = ps_s.tile([P, SK], F32, name="s")
             st["s%d" % j] = s_t
@@ -248,7 +258,7 @@ def tile_multiheadedattention_pa_kernel(tc, q, k, image_feat, W3, b3, out):
                 u, e = n // 2, n % 2
                 nc.tensor.matmul(s_t[:], lhsT=q_b[:, al, u, :, e], rhs=k_b[:, u, :, e], start=(n == 0), stop=(n == 3))
                 if n < 3:
-                    for go, fin in flat[per * n:per * (n + 1)]:
+                    for go, fin in flat[begs[n]:ends[n]]:
                         go()
                         if fin is not None:
                             fin()
@@ -291,22 +301,30 @@ def tile_multiheadedattention_pa_kernel(tc, q, k, image_feat, W3, b3, out):
             nc.vector.quantize_mx(out=imf_c[h][:, P * a:P * a + P].bitcast(FP8X4), scales=imf_s[h][:, P * a:P * a + P],
                                   in_=st["ig%d" % ot][:].rearrange("p o t -> p (o t)"))
 
-        def pv(j):
+        def pv(j, spare_bank=False, on_vector=False, store_alone=False):
             h, a = j // 8, j % 8
             ec, es = st["ec%d" % j]
-            pv_t = ps_p.tile([P, DK], F32, name="pv")
+            if spare_bank:
+                pv_t = ps_s.tile([P, DK], F32, name="s")
+            else:
+                pv_t = ps_p.tile([P, DK], F32, name="pv")
             nc.tensor.matmul_mx(out=pv_t[:], lhsT=ec[:].bitcast(FP8X4), lhsT_scale=es[:], rhs=imf_c[h][:].bitcast(FP8X4),
                                 rhs_scale=imf_s[h][:], start=True, stop=True)
             if a % 2 == 0:
                 st["o"] = op.tile([P, 2, DK], F32, name="o_sb")
-            nc.scalar.activation(out=st["o"][:, a % 2, :], in_=pv_t[:], func=ACT.Copy, scale=st["ri%d" % j][:])
-            if a % 2 == 1:
+            if on_vector:
+                nc.vector.tensor_scalar(out=st["o"][:, a % 2, :], in0=pv_t[:], scalar1=st["ri%d" % j][:], scalar2=None, op0=ALU.mult)
+            else:
+                nc.scalar.activation(out=st["o"][:, a % 2, :], in_=pv_t[:], func=ACT.Copy, scale=st["ri%d" % j][:])
+            if store_alone:
+                nc.sync.dma_start(out=o_v[h][:, a, :], in_=st["o"][:, a % 2, :])
+            elif a % 2 == 1:
                 nc.sync.dma_start(out=o_v[h][:, a - 1:a + 1, :], in_=st["o"][:])
 
         run_jobs([k_job(0, 0), k_job(0, 1), q_job(0)])
         next_pv = 0
         i = 0
-        while next_pv < NQT:
+        while i < NQT:
             jobs = []
             v = i - U_START
             if 0 <= v < NUNIT:
@@ -326,10 +344,12 @@ def tile_multiheadedattention_pa_kernel(tc, q, k, image_feat, W3, b3, out):
             ot_done = i - U_START - NXT - S1_LAG - 1
             if 0 <= ot_done < NOT:
                 quant_imf(ot_done)
+            if i == NQT - 1:
+                softmax_max(i)
             if 0 <= i - E_LAG < NQT:
                 quant_e(i - E_LAG)
                 recip(i - E_LAG)
-            if i < NQT:
+            if i < NQT - 1:
                 softmax_max(i)
             if 0 <= v < NUNIT:
                 quant_u(v)
@@ -347,3 +367,20 @@ def tile_multiheadedattention_pa_kernel(tc, q, k, image_feat, W3, b3, out):
             for j in todo[1:]:
                 pv(j)
             i += 1
+        left = list(range(next_pv, NQT - 2))
+        cut1 = min(len(left), DRAIN_A)
+        cut2 = min(len(left), DRAIN_A + DRAIN_B)
+        run_jobs([e_job(NQT - 2)])
+        for n, j in enumerate(left[:cut1]):
+            pv(j, spare_bank=(n % 3 != 0))
+        quant_e(NQT - 2)
+        recip(NQT - 2)
+        run_jobs([e_job(NQT - 1, ps_t, "tw")])
+        for n, j in enumerate(left[cut1:cut2]):
+            pv(j, spare_bank=((n + cut1) % 3 != 0))
+        quant_e(NQT - 1)
+        recip(NQT - 1)
+        for n, j in enumerate(left[cut2:]):
+            pv(j, spare_bank=((n + cut2) % 3 != 0), on_vector=(n % 2 == 0))
+        pv(NQT - 2, spare_bank=(len(left) % 3 != 0), on_vector=True, store_alone=True)
+        pv(NQT - 1, spare_bank=((len(left) + 1) % 3 != 0), store_alone=True)

@@ -32,7 +32,7 @@ FLOPS = 2 * SK * D * D + 2 * (2 * H * SQ * SK * DK)
 MANUAL = True
 U_START = 1
 PV_PER_BUNCH = 2
-GAP_SPLIT = (0, 1, 0)
+GAP_SPLIT = (1, 1, 1)
 E_LAG = 2
 PV_LAG = 1
 O_BUFS = 6

@@ -76,8 +76,6 @@ def tile_multiheadedattention_pa_kernel(tc, q, k, image_feat, W3, b3, out):
 
         ident_f = const.tile([P, P], F32)
         make_identity(nc, ident_f[:])
-        ident_b = const.tile([P, P], BF16)
-        make_identity(nc, ident_b[:])
         warm = const.tile([P, 1], F32)
         nc.vector.memset(warm[:], 0.0)
         warm2 = const.tile([P, 1], F32)
@@ -184,11 +182,12 @@ def tile_multiheadedattention_pa_kernel(tc, q, k, image_feat, W3, b3, out):
             def fin():
                 if tp == 0:
                     st["kT%d" % h] = tk.tile([P, 1024], F32, name="kT")
-                dst = st["kT%d" % h][:].rearrange("p (u t c) -> p u t c", u=2, t=4)
+                dst = st["kT%d" % h][:].rearrange("p (u x c l) -> p u x c l", u=2, x=2, l=2)[:, :, tp, :, :]
+                src = box["b"][:].rearrange("p u l c -> p u c l")
                 if K_ON_V and not (h == 0 and tp == 1):
-                    nc.vector.tensor_copy(out=dst[:, :, 2 * tp:2 * tp + 2, :], in_=box["b"][:])
+                    nc.vector.tensor_copy(out=dst, in_=src)
                 else:
-                    nc.scalar.copy(out=dst[:, :, 2 * tp:2 * tp + 2, :], in_=box["b"][:])
+                    nc.scalar.copy(out=dst, in_=src)
             return [tr(u, tl) for u in range(2) for tl in range(2)], fin
 
         def q_job(m):
@@ -218,15 +217,16 @@ def tile_multiheadedattention_pa_kernel(tc, q, k, image_feat, W3, b3, out):
             def tr(t):
                 def go():
                     if "b" not in box:
-                        box["b"] = pool.tile([P, 4, P], BF16, name=tag)
-                    nc.tensor.transpose(box["b"][:, t, :], st["e%d" % j][:, P * t:P * t + P], ident_b[:])
+                        box["b"] = pool.tile([P, 2, P], F32, name=tag)
+                    nc.tensor.transpose(box["b"][:, t, :], st["e%d" % j][:].bitcast(F32)[:, P * t:P * t + P], ident_f[:])
                 return go
 
             def fin():
                 eg = ep.tile([P, P, 4], BF16, align_bytes=64, name="eg")
                 st["eg%d" % j] = eg
-                nc.vector.tensor_copy(out=eg[:], in_=box["b"][:].rearrange("p t c -> p c t"))
-            return [tr(t) for t in range(4)], fin
+                eg_w = eg[:].rearrange("p c t -> p (c t)").bitcast(F32).rearrange("p (c x) -> p c x", x=2)
+                nc.vector.tensor_copy(out=eg_w, in_=box["b"][:].rearrange("p x c -> p c x"))
+            return [tr(x) for x in range(2)], fin
 
         def quant_e(j):
             eg = st["eg%d" % j]

@@ -250,7 +250,12 @@ def tile_multiheadedattention_pa_kernel(tc, q, k, image_feat, W3, b3, out):
             ends = [(len(flat) * sum(GAP_SPLIT[:n + 1]) + tot - 1) // tot for n in range(3)]
             begs = [0] + ends[:2]
             h, m, al = j // 8, j // 2, j % 2
-            s_t = ps_s.tile([P, SK], F32, name="s")
+            if j % 3 == 2 and j < U_START + NXT + 4:
+                s_t = ps_p.tile([P, SK], F32, name="pv")
+            elif j % 3 == 2 and j >= U_START + NUNIT + S1_LAG:
+                s_t = ps_a.tile([P, SK], F32, name="acc")
+            else:
+                s_t = ps_s.tile([P, SK], F32, name="s")
             st["s%d" % j] = s_t
             q_b = st["qT%d" % m][:].bitcast(BF16).rearrange("p (a u c e) -> p a u c e", a=2, u=2, e=2)
             k_b = st["kT%d" % h][:].bitcast(BF16).rearrange("p (u c e) -> p u c e", u=2, e=2)
@@ -264,10 +269,12 @@ def tile_multiheadedattention_pa_kernel(tc, q, k, image_feat, W3, b3, out):
                             fin()
 
         def softmax_max(j):
-            mx = small.tile([P, 1], F32, name="mx")
-            nc.vector.tensor_reduce(out=mx[:], in_=st["s%d" % j][:], axis=AX.X, op=ALU.max)
+            st["mx"] = small.tile([P, 1], F32, name="mx")
+            nc.vector.tensor_reduce(out=st["mx"][:], in_=st["s%d" % j][:], axis=AX.X, op=ALU.max)
+
+        def softmax_bias(j):
             nb = small.tile([P, 1], F32, name="nb")
-            nc.vector.tensor_scalar(out=nb[:], in0=mx[:], scalar1=-SCALE, scalar2=None, op0=ALU.mult)
+            nc.vector.tensor_scalar(out=nb[:], in0=st["mx"][:], scalar1=-SCALE, scalar2=None, op0=ALU.mult)
             st["nb%d" % j] = nb
 
         def softmax_exp(j):
@@ -323,12 +330,16 @@ def tile_multiheadedattention_pa_kernel(tc, q, k, image_feat, W3, b3, out):
 
         run_jobs([k_job(0, 0), k_job(0, 1), q_job(0)])
         next_pv = 0
+        owed = None
         i = 0
         while i < NQT:
             jobs = []
+            s1_now = 0 <= i - U_START - NXT - S1_LAG < NOT
             v = i - U_START
             if 0 <= v < NUNIT:
                 jobs.append(u_job(v, 0))
+            if owed is not None:
+                jobs.append(([lambda j=owed: softmax_exp(j)], lambda: None))
             if 0 <= i - E_LAG < NQT:
                 jobs.append(e_job(i - E_LAG))
             if 0 <= v < NUNIT:
@@ -336,7 +347,7 @@ def tile_multiheadedattention_pa_kernel(tc, q, k, image_feat, W3, b3, out):
             if i % 2 == 0 and i // 2 + 1 < NQT // 2:
                 jobs.append(q_job(i // 2 + 1))
             if i % 8 in K_AT and i // 8 + 1 < H:
-                jobs.append(k_job(i // 8 + 1, K_AT.index(i % 8)))
+                jobs.insert(0, k_job(i // 8 + 1, K_AT.index(i % 8)))
             if i < NQT:
                 qk_with_transposes(i, jobs)
             else:
@@ -344,13 +355,12 @@ def tile_multiheadedattention_pa_kernel(tc, q, k, image_feat, W3, b3, out):
             ot_done = i - U_START - NXT - S1_LAG - 1
             if 0 <= ot_done < NOT:
                 quant_imf(ot_done)
-            if i == NQT - 1:
-                softmax_max(i)
-            if 0 <= i - E_LAG < NQT:
+            softmax_max(i)
+            if i >= E_LAG:
                 quant_e(i - E_LAG)
+            softmax_bias(i)
+            if i >= E_LAG:
                 recip(i - E_LAG)
-            if i < NQT - 1:
-                softmax_max(i)
             if 0 <= v < NUNIT:
                 quant_u(v)
             todo = []
@@ -359,8 +369,11 @@ def tile_multiheadedattention_pa_kernel(tc, q, k, image_feat, W3, b3, out):
                 next_pv += 1
             if todo:
                 pv(todo[0])
-            if i < NQT:
+            if s1_now or i == NQT - 1:
                 softmax_exp(i)
+                owed = None
+            else:
+                owed = i
             ot = i - U_START - NXT - S1_LAG
             if 0 <= ot < NOT:
                 stage1(ot)

@@ -34,7 +34,7 @@ U_START = 1
 PV_PER_BUNCH = 2
 GAP_SPLIT = (1, 1, 1)
 E_LAG = 2
-PV_LAG = 1
+PV_LAG = 3
 O_BUFS = 6
 DRAIN_A = 2
 DRAIN_B = 2
@@ -101,10 +101,12 @@ def tile_multiheadedattention_pa_kernel(tc, q, k, image_feat, W3, b3, out):
 
         nc.sync.dma_start(out=k_raw[0][:, 0:1024], in_=k_v[0][:, 0:1024])
         nc.sync.dma_start(out=k_raw[0][:, 1024:2048], in_=k_v[0][:, 1024:2048])
-        nc.sync.dma_start(out=q_raw[0][:, 0:1024], in_=q_v[0][:, 0:1024])
+        for al in range(2):
+            nc.sync.dma_start(out=q_raw[0][:, 512 * al:512 * al + 512], in_=q_v[0][:, 512 * al:512 * al + 512])
         nc.sync.dma_start(out=q_raw[0][:, 1024:2048], in_=q_v[0][:, 1024:2048])
+        nc.sync.dma_start(out=x_raw[0][:], in_=x_v[0])
         load_q2(0)
-        for t in range(NXT):
+        for t in range(1, NXT):
             nc.sync.dma_start(out=x_raw[t][:], in_=x_v[t])
         for ot in range(0, 2):
             load_w(ot)
@@ -210,6 +212,28 @@ def tile_multiheadedattention_pa_kernel(tc, q, k, image_feat, W3, b3, out):
                     nc.scalar.copy(out=st["qT%d" % m][:], in_=box["b"][:].rearrange("p a u c -> p (a u c)"))
             return [tr(al, u) for al in range(2) for u in range(2)], fin
 
+        def first_q_job(al):
+            box = {}
+
+            def tr(u):
+                def go():
+                    if "b" not in box:
+                        box["b"] = (ps_p if al == 0 else ps_a).tile([P, 2, P], F32, name="pv" if al == 0 else "acc")
+                    c0 = 256 * al + P * u
+                    nc.tensor.transpose(box["b"][:, u, :], q_raw[0][:].bitcast(F32)[:, c0:c0 + P], ident_f[:])
+                return go
+
+            def fin():
+                if al == 0:
+                    st["qT0"] = tq.tile([P, 512], F32, name="qT")
+                dst = st["qT0"][:, 256 * al:256 * al + 256]
+                src = box["b"][:].rearrange("p u c -> p (u c)")
+                if al == 0:
+                    nc.vector.tensor_copy(out=dst, in_=src)
+                else:
+                    nc.scalar.copy(out=dst, in_=src)
+            return [tr(u) for u in range(2)], fin
+
         def e_job(j, pool=None, tag="et"):
             pool = pool or ps_e
             box = {}
@@ -308,13 +332,11 @@ def tile_multiheadedattention_pa_kernel(tc, q, k, image_feat, W3, b3, out):
             nc.vector.quantize_mx(out=imf_c[h][:, P * a:P * a + P].bitcast(FP8X4), scales=imf_s[h][:, P * a:P * a + P],
                                   in_=st["ig%d" % ot][:].rearrange("p o t -> p (o t)"))
 
-        def pv(j, spare_bank=False, on_vector=False, store_alone=False):
+        def pv(j, bank=None, on_vector=False, store_alone=False):
             h, a = j // 8, j % 8
             ec, es = st["ec%d" % j]
-            if spare_bank:
-                pv_t = ps_s.tile([P, DK], F32, name="s")
-            else:
-                pv_t = ps_p.tile([P, DK], F32, name="pv")
+            pool, tag = bank or (ps_p, "pv")
+            pv_t = pool.tile([P, DK], F32, name=tag)
             nc.tensor.matmul_mx(out=pv_t[:], lhsT=ec[:].bitcast(FP8X4), lhsT_scale=es[:], rhs=imf_c[h][:].bitcast(FP8X4),
                                 rhs_scale=imf_s[h][:], start=True, stop=True)
             if a % 2 == 0:
@@ -328,7 +350,7 @@ def tile_multiheadedattention_pa_kernel(tc, q, k, image_feat, W3, b3, out):
             elif a % 2 == 1:
                 nc.sync.dma_start(out=o_v[h][:, a - 1:a + 1, :], in_=st["o"][:])
 
-        run_jobs([k_job(0, 0), k_job(0, 1), q_job(0)])
+        run_jobs([k_job(0, 0), k_job(0, 1), first_q_job(0), first_q_job(1)])
         next_pv = 0
         owed = None
         i = 0
@@ -364,11 +386,11 @@ def tile_multiheadedattention_pa_kernel(tc, q, k, image_feat, W3, b3, out):
             if 0 <= v < NUNIT:
                 quant_u(v)
             todo = []
-            while len(todo) < PV_PER_BUNCH and next_pv < NQT and next_pv <= i - E_LAG - PV_LAG and i >= U_START + NXT + 4 * (next_pv // 8) + 3 + S1_LAG + 1:
+            while len(todo) < PV_PER_BUNCH and next_pv <= i - E_LAG - PV_LAG and i >= U_START + NXT + 4 * (next_pv // 8) + 3 + S1_LAG + 1:
                 todo.append(next_pv)
                 next_pv += 1
             if todo:
-                pv(todo[0])
+                pv(todo[0], store_alone=(i == NQT - 1))
             if s1_now or i == NQT - 1:
                 softmax_exp(i)
                 owed = None
@@ -380,20 +402,14 @@ def tile_multiheadedattention_pa_kernel(tc, q, k, image_feat, W3, b3, out):
             for j in todo[1:]:
                 pv(j)
             i += 1
-        left = list(range(next_pv, NQT - 2))
-        cut1 = min(len(left), DRAIN_A)
-        cut2 = min(len(left), DRAIN_A + DRAIN_B)
-        run_jobs([e_job(NQT - 2)])
-        for n, j in enumerate(left[:cut1]):
-            pv(j, spare_bank=(n % 3 != 0))
-        quant_e(NQT - 2)
-        recip(NQT - 2)
-        run_jobs([e_job(NQT - 1, ps_t, "tw")])
-        for n, j in enumerate(left[cut1:cut2]):
-            pv(j, spare_bank=((n + cut1) % 3 != 0))
-        quant_e(NQT - 1)
-        recip(NQT - 1)
-        for n, j in enumerate(left[cut2:]):
-            pv(j, spare_bank=((n + cut2) % 3 != 0), on_vector=(n % 2 == 0))
-        pv(NQT - 2, spare_bank=(len(left) % 3 != 0), on_vector=True, store_alone=True)
-        pv(NQT - 1, spare_bank=((len(left) + 1) % 3 != 0), store_alone=True)
+        n_last = NQT - 1
+        run_jobs([e_job(n_last - 1)])
+        quant_e(n_last - 1)
+        for n, j in enumerate(range(next_pv, n_last - 1)):
+            pv(j, bank=(ps_t, "tw"), on_vector=(n == 0), store_alone=True)
+        recip(n_last - 1)
+        run_jobs([e_job(n_last)])
+        quant_e(n_last)
+        recip(n_last)
+        pv(n_last - 1, bank=(ps_s, "s"), on_vector=True, store_alone=True)
+        pv(n_last, bank=(ps_s, "s"), store_alone=True)

@@ -25,7 +25,7 @@ NQT = H * SQ // P
 NOT = D // P
 NXT = SK // P
 NUNIT = NXT + NOT
-W_BUFS = 10
+W_BUFS = 16
 SCALE = 1.0 / math.sqrt(DK)
 FLOPS = 2 * SK * D * D + 2 * (2 * H * SQ * SK * DK)
 
@@ -34,10 +34,13 @@ U_START = 1
 PV_PER_BUNCH = 2
 GAP_SPLIT = (1, 1, 1)
 E_LAG = 2
-PV_LAG = 3
-O_BUFS = 6
+PV_LAG = 1
+O_BUFS = 5
 DRAIN_A = 2
 DRAIN_B = 2
+V_HEADS = (3,)
+LATE_FROM = 5
+VEC_FROM = 15
 K_AT = (5, 7)
 K_ON_V = True
 Q_ON_V = 0
@@ -58,6 +61,7 @@ def tile_multiheadedattention_pa_kernel(tc, q, k, image_feat, W3, b3, out):
         wq = ctx.enter_context(tc.tile_pool(name="wq", bufs=S1_LAG + 2))
         tq = ctx.enter_context(tc.tile_pool(name="tq", bufs=3))
         tk = ctx.enter_context(tc.tile_pool(name="tk", bufs=2))
+        tv = ctx.enter_context(tc.tile_pool(name="tv", bufs=2))
         ep = ctx.enter_context(tc.tile_pool(name="ep", bufs=E_LAG + 2))
         eq = ctx.enter_context(tc.tile_pool(name="eq", bufs=14))
         small = ctx.enter_context(tc.tile_pool(name="small", bufs=3))
@@ -69,10 +73,13 @@ def tile_multiheadedattention_pa_kernel(tc, q, k, image_feat, W3, b3, out):
         ps_p = ctx.enter_context(tc.psum_pool(name="ps_p", bufs=1))
 
         q_v = q[0].rearrange("h (p a) d -> h p (a d)", a=8)
-        k_v = k[0].rearrange("h (p t) d -> h p (t d)", t=4)
-        x_v = image_feat[0].rearrange("(p t) i -> t p i", t=4)
+        k_v = k[0].rearrange("h (t p) d -> h p t d", p=P)
+        x_v = image_feat[0].rearrange("(x p l) i -> x l p i", x=2, l=2)
+        kb_v = k[0].rearrange("h (b c) d -> h c b d", c=32)
+        qb_v = q[0].rearrange("h (b c l) d -> h l c b d", c=32, l=2)
         w_v = W3.rearrange("(a p) i -> a p i", p=P)
-        o_v = out[0].rearrange("h (p a) d -> h p a d", a=8)
+        o_t = out[0].rearrange("h (p a) d -> h p a d", a=8)
+        o_b = out[0].rearrange("h (m p l) d -> h m p l d", m=4, l=2)
 
         ident_f = const.tile([P, P], F32)
         make_identity(nc, ident_f[:])
@@ -81,14 +88,26 @@ def tile_multiheadedattention_pa_kernel(tc, q, k, image_feat, W3, b3, out):
         warm2 = const.tile([P, 1], F32)
         nc.scalar.activation(out=warm2[:], in_=warm[:], func=ACT.Exp)
 
-        k_raw = [raw.tile([P, 2048], BF16, name="k_raw%d" % h) for h in range(H)]
-        q_raw = [raw.tile([P, 4096], BF16, name="q_raw%d" % h) for h in range(H)]
+        k_raw = [raw.tile([P, 2048], BF16, align_bytes=64, name="k_raw%d" % h) for h in range(H)]
+        q_raw = [raw.tile([P, 4096], BF16, align_bytes=64, name="q_raw%d" % h) for h in range(H)]
         x_raw = [raw.tile([P, 2048], BF16, name="x_raw%d" % t) for t in range(NXT)]
         bias = const.tile([P, D], BF16)
         w_raw = {}
 
+        def vector_head_loads(h):
+            pairs = []
+            for w in range(2):
+                for l in range(2):
+                    for qd in (0, 2, 1, 3):
+                        c0 = 2048 * w + 1024 * l
+                        pairs.append((q_raw[h][32 * qd:32 * qd + 32, c0:c0 + 1024].rearrange("c (b d) -> c b d", d=64),
+                                      qb_v[h][l][:, :, P * qd + 64 * w:P * qd + 64 * w + 64]))
+            for qd in (0, 2, 1, 3):
+                pairs.append((k_raw[h][32 * qd:32 * qd + 32, :].rearrange("c (b d) -> c b d", d=P), kb_v[h][:, :, P * qd:P * qd + P]))
+            return pairs
+
         def load_kq(h):
-            nc.sync.dma_start(out=k_raw[h][:], in_=k_v[h])
+            nc.sync.dma_start(out=k_raw[h][:].rearrange("p (t d) -> p t d", t=4), in_=k_v[h])
             nc.sync.dma_start(out=q_raw[h][:, 0:2048], in_=q_v[h][:, 0:2048])
 
         def load_q2(h):
@@ -99,15 +118,15 @@ def tile_multiheadedattention_pa_kernel(tc, q, k, image_feat, W3, b3, out):
             nc.sync.dma_start(out=w_t[:], in_=w_v[ot])
             w_raw[ot] = w_t
 
-        nc.sync.dma_start(out=k_raw[0][:, 0:1024], in_=k_v[0][:, 0:1024])
-        nc.sync.dma_start(out=k_raw[0][:, 1024:2048], in_=k_v[0][:, 1024:2048])
+        for t in (0, 2):
+            nc.sync.dma_start(out=k_raw[0][:, 512 * t:512 * t + 1024].rearrange("p (t d) -> p t d", t=2), in_=k_v[0][:, t:t + 2, :])
         for al in range(2):
             nc.sync.dma_start(out=q_raw[0][:, 512 * al:512 * al + 512], in_=q_v[0][:, 512 * al:512 * al + 512])
         nc.sync.dma_start(out=q_raw[0][:, 1024:2048], in_=q_v[0][:, 1024:2048])
-        nc.sync.dma_start(out=x_raw[0][:], in_=x_v[0])
+        nc.sync.dma_start(out=x_raw[0][:], in_=x_v[0][0])
         load_q2(0)
         for t in range(1, NXT):
-            nc.sync.dma_start(out=x_raw[t][:], in_=x_v[t])
+            nc.sync.dma_start(out=x_raw[t][:], in_=x_v[t // 2][t % 2])
         for ot in range(0, 2):
             load_w(ot)
         load_kq(1)
@@ -121,8 +140,7 @@ def tile_multiheadedattention_pa_kernel(tc, q, k, image_feat, W3, b3, out):
         load_q2(2)
         for ot in range(8, W_BUFS):
             load_w(ot)
-        load_kq(3)
-        load_q2(3)
+        late = vector_head_loads(3)
 
         xc = keep.tile([P, NXT, 4, P], U32, align_bytes=64)
         xs = keep.tile([P, NXT, 4, P], U8, align_bytes=64)
@@ -183,14 +201,26 @@ def tile_multiheadedattention_pa_kernel(tc, q, k, image_feat, W3, b3, out):
 
             def fin():
                 if tp == 0:
-                    st["kT%d" % h] = tk.tile([P, 1024], F32, name="kT")
-                dst = st["kT%d" % h][:].rearrange("p (u x c l) -> p u x c l", u=2, x=2, l=2)[:, :, tp, :, :]
-                src = box["b"][:].rearrange("p u l c -> p u c l")
+                    st["kT%d" % h] = tk.tile([P, 1024], F32, align_bytes=64, name="kT")
+                dst = st["kT%d" % h][:].rearrange("p (u t c) -> p u t c", u=2, t=4)[:, :, 2 * tp:2 * tp + 2, :]
+                src = box["b"][:]
                 if K_ON_V and not (h == 0 and tp == 1):
                     nc.vector.tensor_copy(out=dst, in_=src)
                 else:
                     nc.scalar.copy(out=dst, in_=src)
             return [tr(u, tl) for u in range(2) for tl in range(2)], fin
+
+        def k_turn(h, b2):
+            if b2 == 0:
+                st["kT%d" % h] = tk.tile([P, 1024], F32, align_bytes=64, name="kT")
+            cols = slice(512 * b2, 512 * b2 + 512)
+            nc.vector.transpose(st["kT%d" % h][:, cols], k_raw[h][:].bitcast(F32)[:, cols])
+
+        def q_turn(h, w, l):
+            if w == 0:
+                st["qV%d_%d" % (h, l)] = tv.tile([P, 1024], F32, align_bytes=64, name="qV")
+            c0 = 1024 * w + 512 * l
+            nc.vector.transpose(st["qV%d_%d" % (h, l)][:, 512 * w:512 * w + 512], q_raw[h][:].bitcast(F32)[:, c0:c0 + 512])
 
         def q_job(m):
             h, a0 = (2 * m) // 8, (2 * m) % 8
@@ -281,11 +311,16 @@ def tile_multiheadedattention_pa_kernel(tc, q, k, image_feat, W3, b3, out):
             else:
                 s_t = ps_s.tile([P, SK], F32, name="s")
             st["s%d" % j] = s_t
-            q_b = st["qT%d" % m][:].bitcast(BF16).rearrange("p (a u c e) -> p a u c e", a=2, u=2, e=2)
-            k_b = st["kT%d" % h][:].bitcast(BF16).rearrange("p (u c e) -> p u c e", u=2, e=2)
+            if h in V_HEADS:
+                q_b = st["qV%d_%d" % (h, j % 2)][:].bitcast(BF16).rearrange("p (u m c e) -> p m u c e", m=4, u=2, e=2)[:, (j % 8) // 2]
+                k_b = st["kT%d" % h][:].bitcast(BF16).rearrange("p (b u c e) -> p u b c e", b=16, u=2, e=2)
+            else:
+                q_b = st["qT%d" % m][:].bitcast(BF16).rearrange("p (a u c e) -> p a u c e", a=2, u=2, e=2)[:, al]
+                k_b = st["kT%d" % h][:].bitcast(BF16).rearrange("p (u c e) -> p u c e", u=2, e=2)
             for n in range(4):
                 u, e = n // 2, n % 2
-                nc.tensor.matmul(s_t[:], lhsT=q_b[:, al, u, :, e], rhs=k_b[:, u, :, e], start=(n == 0), stop=(n == 3))
+                rhs = k_b[:, u, :, :, e] if h in V_HEADS else k_b[:, u, :, e]
+                nc.tensor.matmul(s_t[:], lhsT=q_b[:, u, :, e], rhs=rhs, start=(n == 0), stop=(n == 3))
                 if n < 3:
                     for go, fin in flat[begs[n]:ends[n]]:
                         go()
@@ -345,18 +380,24 @@ def tile_multiheadedattention_pa_kernel(tc, q, k, image_feat, W3, b3, out):
                 nc.vector.tensor_scalar(out=st["o"][:, a % 2, :], in0=pv_t[:], scalar1=st["ri%d" % j][:], scalar2=None, op0=ALU.mult)
             else:
                 nc.scalar.activation(out=st["o"][:, a % 2, :], in_=pv_t[:], func=ACT.Copy, scale=st["ri%d" % j][:])
+            o_pair = o_b[h][a // 2] if h in V_HEADS else o_t[h][:, a - a % 2:a - a % 2 + 2, :]
             if store_alone:
-                nc.sync.dma_start(out=o_v[h][:, a, :], in_=st["o"][:, a % 2, :])
+                nc.sync.dma_start(out=o_pair[:, a % 2, :], in_=st["o"][:, a % 2, :])
             elif a % 2 == 1:
-                nc.sync.dma_start(out=o_v[h][:, a - 1:a + 1, :], in_=st["o"][:])
+                nc.sync.dma_start(out=o_pair, in_=st["o"][:])
 
         run_jobs([k_job(0, 0), k_job(0, 1), first_q_job(0), first_q_job(1)])
+        turns = [lambda: q_turn(3, 0, 0), lambda: q_turn(3, 0, 1), lambda: q_turn(3, 1, 0), lambda: q_turn(3, 1, 1),
+                 lambda: k_turn(3, 0), lambda: k_turn(3, 1)]
         next_pv = 0
         owed = None
         i = 0
         while i < NQT:
-            jobs = []
             s1_now = 0 <= i - U_START - NXT - S1_LAG < NOT
+            if i >= LATE_FROM:
+                for dst, src in late[2 * (i - LATE_FROM):2 * (i - LATE_FROM) + 2]:
+                    nc.sync.dma_start(out=dst, in_=src)
+            jobs = []
             v = i - U_START
             if 0 <= v < NUNIT:
                 jobs.append(u_job(v, 0))
@@ -366,9 +407,9 @@ def tile_multiheadedattention_pa_kernel(tc, q, k, image_feat, W3, b3, out):
                 jobs.append(e_job(i - E_LAG))
             if 0 <= v < NUNIT:
                 jobs.append(u_job(v, 1))
-            if i % 2 == 0 and i // 2 + 1 < NQT // 2:
+            if i % 2 == 0 and i // 2 + 1 < NQT // 2 and (i + 2) // 8 not in V_HEADS:
                 jobs.append(q_job(i // 2 + 1))
-            if i % 8 in K_AT and i // 8 + 1 < H:
+            if i % 8 in K_AT and i // 8 + 1 < H and i // 8 + 1 not in V_HEADS:
                 jobs.insert(0, k_job(i // 8 + 1, K_AT.index(i % 8)))
             if i < NQT:
                 qk_with_transposes(i, jobs)
@@ -390,7 +431,7 @@ def tile_multiheadedattention_pa_kernel(tc, q, k, image_feat, W3, b3, out):
                 todo.append(next_pv)
                 next_pv += 1
             if todo:
-                pv(todo[0], store_alone=(i == NQT - 1))
+                pv(todo[0])
             if s1_now or i == NQT - 1:
                 softmax_exp(i)
                 owed = None
@@ -401,13 +442,15 @@ def tile_multiheadedattention_pa_kernel(tc, q, k, image_feat, W3, b3, out):
                 stage1(ot)
             for j in todo[1:]:
                 pv(j)
+            if 0 <= i - VEC_FROM < len(turns):
+                turns[i - VEC_FROM]()
             i += 1
         n_last = NQT - 1
         run_jobs([e_job(n_last - 1)])
         quant_e(n_last - 1)
-        for n, j in enumerate(range(next_pv, n_last - 1)):
-            pv(j, bank=(ps_t, "tw"), on_vector=(n == 0), store_alone=True)
         recip(n_last - 1)
+        for j in range(next_pv, n_last - 1):
+            pv(j, bank=(ps_t, "tw"))
         run_jobs([e_job(n_last)])
         quant_e(n_last)
         recip(n_last)

@@ -25,7 +25,7 @@ NQT = H * SQ // P
 NOT = D // P
 NXT = SK // P
 NUNIT = NXT + NOT
-W_BUFS = 16
+W_BUFS = 15
 SCALE = 1.0 / math.sqrt(DK)
 FLOPS = 2 * SK * D * D + 2 * (2 * H * SQ * SK * DK)
 
@@ -40,7 +40,7 @@ DRAIN_A = 2
 DRAIN_B = 2
 V_HEADS = (3,)
 LATE_FROM = 5
-VEC_FROM = 15
+VEC_FROM = 14
 K_AT = (5, 7)
 K_ON_V = True
 Q_ON_V = 0
@@ -142,10 +142,10 @@ def tile_multiheadedattention_pa_kernel(tc, q, k, image_feat, W3, b3, out):
             load_w(ot)
         late = vector_head_loads(3)
 
-        xc = keep.tile([P, NXT, 4, P], U32, align_bytes=64)
-        xs = keep.tile([P, NXT, 4, P], U8, align_bytes=64)
-        imf_c = [keep.tile([P, DK], U32, align_bytes=64, name="imf_c%d" % h) for h in range(H)]
-        imf_s = [keep.tile([P, DK], U8, align_bytes=64, name="imf_s%d" % h) for h in range(H)]
+        xc = keep.tile([P, NXT, 4, P], U32, align_bytes=256)
+        xs = keep.tile([P, NXT, 4, P], U8, align_bytes=256)
+        imf_c = [keep.tile([P, DK], U32, align_bytes=256, name="imf_c%d" % h) for h in range(H)]
+        imf_s = [keep.tile([P, DK], U8, align_bytes=256, name="imf_s%d" % h) for h in range(H)]
 
         st = {}
 
@@ -181,8 +181,8 @@ def tile_multiheadedattention_pa_kernel(tc, q, k, image_feat, W3, b3, out):
                 c_ap = xc[:, v, :, :].rearrange("p g c -> p (g c)")
                 s_ap = xs[:, v, :, :].rearrange("p g c -> p (g c)")
             else:
-                wc = wq.tile([P, 4 * P], U32, align_bytes=64, name="wc")
-                ws = wq.tile([P, 4 * P], U8, align_bytes=64, name="ws")
+                wc = wq.tile([P, 4 * P], U32, align_bytes=256, name="wc")
+                ws = wq.tile([P, 4 * P], U8, align_bytes=256, name="ws")
                 st["wc%d" % (v - NXT)] = (wc, ws)
                 c_ap = wc[:]
                 s_ap = ws[:]
@@ -284,8 +284,8 @@ def tile_multiheadedattention_pa_kernel(tc, q, k, image_feat, W3, b3, out):
 
         def quant_e(j):
             eg = st["eg%d" % j]
-            ec = eq.tile([P, P], U32, align_bytes=64, name="ec")
-            es = eq.tile([P, P], U8, align_bytes=64, name="es")
+            ec = eq.tile([P, P], U32, align_bytes=256, name="ec")
+            es = eq.tile([P, P], U8, align_bytes=256, name="es")
             st["ec%d" % j] = (ec, es)
             nc.vector.quantize_mx(out=ec[:].bitcast(FP8X4), scales=es[:], in_=eg[:].rearrange("p c t -> p (c t)"))
 
@@ -431,7 +431,7 @@ def tile_multiheadedattention_pa_kernel(tc, q, k, image_feat, W3, b3, out):
                 todo.append(next_pv)
                 next_pv += 1
             if todo:
-                pv(todo[0])
+                pv(todo[0], store_alone=(i == NQT - 1))
             if s1_now or i == NQT - 1:
                 softmax_exp(i)
                 owed = None
@@ -450,9 +450,20 @@ def tile_multiheadedattention_pa_kernel(tc, q, k, image_feat, W3, b3, out):
         quant_e(n_last - 1)
         recip(n_last - 1)
         for j in range(next_pv, n_last - 1):
-            pv(j, bank=(ps_t, "tw"))
+            pv(j, bank=(ps_t, "tw"), store_alone=True)
         run_jobs([e_job(n_last)])
         quant_e(n_last)
         recip(n_last)
-        pv(n_last - 1, bank=(ps_s, "s"), on_vector=True, store_alone=True)
-        pv(n_last, bank=(ps_s, "s"), store_alone=True)
+        pv(n_last - 1, bank=(ps_a, "acc"), store_alone=True)
+        ec, es = st["ec%d" % n_last]
+        for half in range(2):
+            cols = slice(256 * half, 256 * half + 256)
+            half_t = ps_s.tile([P, 256], F32, name="s")
+            nc.tensor.matmul_mx(out=half_t[:], lhsT=ec[:].bitcast(FP8X4), lhsT_scale=es[:], rhs=imf_c[H - 1][:, cols].bitcast(FP8X4),
+                                rhs_scale=imf_s[H - 1][:, cols], start=True, stop=True)
+            dst = st["o"][:, 1, cols]
+            if half == 0:
+                nc.vector.tensor_scalar(out=dst, in0=half_t[:], scalar1=st["ri%d" % n_last][:], scalar2=None, op0=ALU.mult)
+            else:
+                nc.scalar.activation(out=dst, in_=half_t[:], func=ACT.Copy, scale=st["ri%d" % n_last][:])
+            nc.sync.dma_start(out=o_b[H - 1][8 // 2 - 1][:, 1, cols], in_=dst)

import math
from contextlib import ExitStack

import concourse.bass as bass
import concourse.mybir as mybir
import concourse.tile as tile
from concourse.masks import make_identity

F32 = mybir.dt.float32
BF16 = mybir.dt.bfloat16
U32 = mybir.dt.uint32
U8 = mybir.dt.uint8
FP8X4 = mybir.dt.float8_e4m3fn_x4
ACT = mybir.ActivationFunctionType
ALU = mybir.AluOpType
AX = mybir.AxisListType

P = 128
H = 4
SQ = 1024
SK = 512
DK = 512
D = 2048
NQT = H * SQ // P
NOT = D // P
NXT = SK // P
NUNIT = NXT + NOT
W_BUFS = 15
SCALE = 1.0 / math.sqrt(DK)
FLOPS = 2 * SK * D * D + 2 * (2 * H * SQ * SK * DK)

MANUAL = True
U_START = 1
PV_PER_BUNCH = 2
GAP_SPLIT = (1, 1, 1)
E_LAG = 2
PV_LAG = 1
O_BUFS = 5
DRAIN_A = 2
DRAIN_B = 2
V_HEADS = (3,)
LATE_FROM = 5
VEC_FROM = 14
K_AT = (5, 7)
K_ON_V = True
Q_ON_V = 0
U_ON_V = 0
S1_LAG = 1


def tile_multiheadedattention_pa_kernel(tc, q, k, image_feat, W3, b3, out):
    nc = tc.nc
    with ExitStack() as ctx:
        if MANUAL:
            ctx.enter_context(tc.manual_schedule())
        const = ctx.enter_context(tc.tile_pool(name="const", bufs=1))
        raw = ctx.enter_context(tc.tile_pool(name="raw", bufs=1))
        wraw = ctx.enter_context(tc.tile_pool(name="wraw", bufs=W_BUFS))
        keep = ctx.enter_context(tc.tile_pool(name="keep", bufs=1))
        grp = ctx.enter_context(tc.tile_pool(name="grp", bufs=3))
        wq = ctx.enter_context(tc.tile_pool(name="wq", bufs=S1_LAG + 2))
        tq = ctx.enter_context(tc.tile_pool(name="tq", bufs=3))
        tk = ctx.enter_context(tc.tile_pool(name="tk", bufs=2))
        tv = ctx.enter_context(tc.tile_pool(name="tv", bufs=2))
        ep = ctx.enter_context(tc.tile_pool(name="ep", bufs=E_LAG + 2))
        eq = ctx.enter_context(tc.tile_pool(name="eq", bufs=14))
        small = ctx.enter_context(tc.tile_pool(name="small", bufs=3))
        op = ctx.enter_context(tc.tile_pool(name="op", bufs=O_BUFS))
        ps_s = ctx.enter_context(tc.psum_pool(name="ps_s", bufs=2))
        ps_t = ctx.enter_context(tc.psum_pool(name="ps_t", bufs=3))
        ps_e = ctx.enter_context(tc.psum_pool(name="ps_e", bufs=1))
        ps_a = ctx.enter_context(tc.psum_pool(name="ps_a", bufs=1))
        ps_p = ctx.enter_context(tc.psum_pool(name="ps_p", bufs=1))

        q_v = q[0].rearrange("h (p a) d -> h p (a d)", a=8)
        k_v = k[0].rearrange("h (t p) d -> h p t d", p=P)
        x_v = image_feat[0].rearrange("(x p l) i -> x l p i", x=2, l=2)
        kb_v = k[0].rearrange("h (b c) d -> h c b d", c=32)
        qb_v = q[0].rearrange("h (b c l) d -> h l c b d", c=32, l=2)
        w_v = W3.rearrange("(a p) i -> a p i", p=P)
        o_t = out[0].rearrange("h (p a) d -> h p a d", a=8)
        o_b = out[0].rearrange("h (m p l) d -> h m p l d", m=4, l=2)

        ident_f = const.tile([P, P], F32)
        make_identity(nc, ident_f[:])
        warm = const.tile([P, 1], F32)
        nc.vector.memset(warm[:], 0.0)
        warm2 = const.tile([P, 1], F32)
        nc.scalar.activation(out=warm2[:], in_=warm[:], func=ACT.Exp)

        k_raw = [raw.tile([P, 2048], BF16, align_bytes=64, name="k_raw%d" % h) for h in range(H)]
        q_raw = [raw.tile([P, 4096], BF16, align_bytes=64, name="q_raw%d" % h) for h in range(H)]
        x_raw = [raw.tile([P, 2048], BF16, name="x_raw%d" % t) for t in range(NXT)]
        bias = const.tile([P, D], BF16)
        w_raw = {}

        def vector_head_loads(h):
            pairs = []
            for w in range(2):
                for l in range(2):
                    for qd in (0, 2, 1, 3):
                        c0 = 2048 * w + 1024 * l
                        pairs.append((q_raw[h][32 * qd:32 * qd + 32, c0:c0 + 1024].rearrange("c (b d) -> c b d", d=64),
                                      qb_v[h][l][:, :, P * qd + 64 * w:P * qd + 64 * w + 64]))
            for qd in (0, 2, 1, 3):
                pairs.append((k_raw[h][32 * qd:32 * qd + 32, :].rearrange("c (b d) -> c b d", d=P), kb_v[h][:, :, P * qd:P * qd + P]))
            return pairs

        def load_kq(h):
            nc.sync.dma_start(out=k_raw[h][:].rearrange("p (t d) -> p t d", t=4), in_=k_v[h])
            nc.sync.dma_start(out=q_raw[h][:, 0:2048], in_=q_v[h][:, 0:2048])

        def load_q2(h):
            nc.sync.dma_start(out=q_raw[h][:, 2048:4096], in_=q_v[h][:, 2048:4096])

        def load_w(ot):
            w_t = wraw.tile([P, 2048], BF16, name="w_raw")
            nc.sync.dma_start(out=w_t[:], in_=w_v[ot])
            w_raw[ot] = w_t

        for t in (0, 2):
            nc.sync.dma_start(out=k_raw[0][:, 512 * t:512 * t + 1024].rearrange("p (t d) -> p t d", t=2), in_=k_v[0][:, t:t + 2, :])
        for al in range(2):
            nc.sync.dma_start(out=q_raw[0][:, 512 * al:512 * al + 512], in_=q_v[0][:, 512 * al:512 * al + 512])
        nc.sync.dma_start(out=q_raw[0][:, 1024:2048], in_=q_v[0][:, 1024:2048])
        nc.sync.dma_start(out=x_raw[0][:], in_=x_v[0][0])
        load_q2(0)
        for t in range(1, NXT):
            nc.sync.dma_start(out=x_raw[t][:], in_=x_v[t // 2][t % 2])
        for ot in range(0, 2):
            load_w(ot)
        load_kq(1)
        for ot in range(2, 4):
            load_w(ot)
        nc.sync.dma_start(out=bias[:], in_=b3.partition_broadcast(P))
        load_q2(1)
        for ot in range(4, 8):
            load_w(ot)
        load_kq(2)
        load_q2(2)
        for ot in range(8, W_BUFS):
            load_w(ot)
        late = vector_head_loads(3)

        xc = keep.tile([P, NXT, 4, P], U32, align_bytes=256)
        xs = keep.tile([P, NXT, 4, P], U8, align_bytes=256)
        imf_c = [keep.tile([P, DK], U32, align_bytes=256, name="imf_c%d" % h) for h in range(H)]
        imf_s = [keep.tile([P, DK], U8, align_bytes=256, name="imf_s%d" % h) for h in range(H)]

        st = {}

        def unit_raw(v):
            return x_raw[v] if v < NXT else w_raw[v - NXT]

        def u_job(v, gp):
            box = {}

            def tr(gl, u):
                def go():
                    if "b" not in box:
                        box["b"] = ps_t.tile([P, 2, 2, P], F32, name="tw")
                    c0 = P * (2 * (2 * gp + gl) + u)
                    nc.tensor.transpose(box["b"][:, gl, u, :], unit_raw(v)[:].bitcast(F32)[:, c0:c0 + P], ident_f[:])
                return go

            def fin():
                if gp == 0:
                    st["g%d" % v] = grp.tile([P, 2048], BF16, align_bytes=64, name="grouped")
                g_f = st["g%d" % v][:].bitcast(F32).rearrange("p (g c u) -> p g c u", g=4, u=2)
                if U_ON_V and gp == 0 and v % U_ON_V == 0:
                    nc.vector.tensor_copy(out=g_f[:, 2 * gp:2 * gp + 2, :, :], in_=box["b"][:].rearrange("p g u c -> p g c u"))
                else:
                    nc.scalar.copy(out=g_f[:, 2 * gp:2 * gp + 2, :, :], in_=box["b"][:].rearrange("p g u c -> p g c u"))
                if gp == 1 and v >= NXT and v - NXT + W_BUFS < NOT:
                    load_w(v - NXT + W_BUFS)
            return [tr(gl, u) for gl in range(2) for u in range(2)], fin

        def quant_u(v):
            g_t = st["g%d" % v]
            if v < NXT:
                c_ap = xc[:, v, :, :].rearrange("p g c -> p (g c)")
                s_ap = xs[:, v, :, :].rearrange("p g c -> p (g c)")
            else:
                wc = wq.tile([P, 4 * P], U32, align_bytes=256, name="wc")
                ws = wq.tile([P, 4 * P], U8, align_bytes=256, name="ws")
                st["wc%d" % (v - NXT)] = (wc, ws)
                c_ap = wc[:]
                s_ap = ws[:]
            nc.vector.quantize_mx(out=c_ap.bitcast(FP8X4), scales=s_ap, in_=g_t[:])

        def k_job(h, tp):
            box = {}

            def tr(u, tl):
                def go():
                    if "b" not in box:
                        box["b"] = ps_t.tile([P, 2, 2, P], F32, name="tw")
                    c0 = 256 * (2 * tp + tl) + P * u
                    nc.tensor.transpose(box["b"][:, u, tl, :], k_raw[h][:].bitcast(F32)[:, c0:c0 + P], ident_f[:])
                return go

            def fin():
                if tp == 0:
                    st["kT%d" % h] = tk.tile([P, 1024], F32, align_bytes=64, name="kT")
                dst = st["kT%d" % h][:].rearrange("p (u t c) -> p u t c", u=2, t=4)[:, :, 2 * tp:2 * tp + 2, :]
                src = box["b"][:]
                if K_ON_V and not (h == 0 and tp == 1):
                    nc.vector.tensor_copy(out=dst, in_=src)
                else:
                    nc.scalar.copy(out=dst, in_=src)
            return [tr(u, tl) for u in range(2) for tl in range(2)], fin

        def k_turn(h, b2):
            if b2 == 0:
                st["kT%d" % h] = tk.tile([P, 1024], F32, align_bytes=64, name="kT")
            cols = slice(512 * b2, 512 * b2 + 512)
            nc.vector.transpose(st["kT%d" % h][:, cols], k_raw[h][:].bitcast(F32)[:, cols])

        def q_turn(h, w, l):
            if w == 0:
                st["qV%d_%d" % (h, l)] = tv.tile([P, 1024], F32, align_bytes=64, name="qV")
            c0 = 1024 * w + 512 * l
            nc.vector.transpose(st["qV%d_%d" % (h, l)][:, 512 * w:512 * w + 512], q_raw[h][:].bitcast(F32)[:, c0:c0 + 512])

        def q_job(m):
            h, a0 = (2 * m) // 8, (2 * m) % 8
            box = {}

            def tr(al, u):
                def go():
                    if "b" not in box:
                        box["b"] = ps_t.tile([P, 2, 2, P], F32, name="tw")
                    c0 = 256 * (a0 + al) + P * u
                    nc.tensor.transpose(box["b"][:, al, u, :], q_raw[h][:].bitcast(F32)[:, c0:c0 + P], ident_f[:])
                return go

            def fin():
                st["qT%d" % m] = tq.tile([P, 512], F32, name="qT")
                if m == 0 or (Q_ON_V and m % Q_ON_V == 0):
                    nc.vector.tensor_copy(out=st["qT%d" % m][:], in_=box["b"][:].rearrange("p a u c -> p (a u c)"))
                else:
                    nc.scalar.copy(out=st["qT%d" % m][:], in_=box["b"][:].rearrange("p a u c -> p (a u c)"))
            return [tr(al, u) for al in range(2) for u in range(2)], fin

        def first_q_job(al):
            box = {}

            def tr(u):
                def go():
                    if "b" not in box:
                        box["b"] = (ps_p if al == 0 else ps_a).tile([P, 2, P], F32, name="pv" if al == 0 else "acc")
                    c0 = 256 * al + P * u
                    nc.tensor.transpose(box["b"][:, u, :], q_raw[0][:].bitcast(F32)[:, c0:c0 + P], ident_f[:])
                return go

            def fin():
                if al == 0:
                    st["qT0"] = tq.tile([P, 512], F32, name="qT")
                dst = st["qT0"][:, 256 * al:256 * al + 256]
                src = box["b"][:].rearrange("p u c -> p (u c)")
                if al == 0:
                    nc.vector.tensor_copy(out=dst, in_=src)
                else:
                    nc.scalar.copy(out=dst, in_=src)
            return [tr(u) for u in range(2)], fin

        def e_job(j, pool=None, tag="et"):
            pool = pool or ps_e
            box = {}

            def tr(t):
                def go():
                    if "b" not in box:
                        box["b"] = pool.tile([P, 2, P], F32, name=tag)
                    nc.tensor.transpose(box["b"][:, t, :], st["e%d" % j][:].bitcast(F32)[:, P * t:P * t + P], ident_f[:])
                return go

            def fin():
                eg = ep.tile([P, P, 4], BF16, align_bytes=64, name="eg")
                st["eg%d" % j] = eg
                eg_w = eg[:].rearrange("p c t -> p (c t)").bitcast(F32).rearrange("p (c x) -> p c x", x=2)
                nc.vector.tensor_copy(out=eg_w, in_=box["b"][:].rearrange("p x c -> p c x"))
            return [tr(x) for x in range(2)], fin

        def quant_e(j):
            eg = st["eg%d" % j]
            ec = eq.tile([P, P], U32, align_bytes=256, name="ec")
            es = eq.tile([P, P], U8, align_bytes=256, name="es")
            st["ec%d" % j] = (ec, es)
            nc.vector.quantize_mx(out=ec[:].bitcast(FP8X4), scales=es[:], in_=eg[:].rearrange("p c t -> p (c t)"))

        def run_jobs(jobs):
            for trs, fin in jobs:
                for go in trs:
                    go()
                fin()

        def qk_with_transposes(j, jobs):
            flat = []
            for trs, fin in jobs:
                for n, go in enumerate(trs):
                    flat.append((go, fin if n == len(trs) - 1 else None))
            tot = sum(GAP_SPLIT)
            ends = [(len(flat) * sum(GAP_SPLIT[:n + 1]) + tot - 1) // tot for n in range(3)]
            begs = [0] + ends[:2]
            h, m, al = j // 8, j // 2, j % 2
            if j % 3 == 2 and j < U_START + NXT + 4:
                s_t = ps_p.tile([P, SK], F32, name="pv")
            elif j % 3 == 2 and j >= U_START + NUNIT + S1_LAG:
                s_t = ps_a.tile([P, SK], F32, name="acc")
            else:
                s_t = ps_s.tile([P, SK], F32, name="s")
            st["s%d" % j] = s_t
            if h in V_HEADS:
                q_b = st["qV%d_%d" % (h, j % 2)][:].bitcast(BF16).rearrange("p (u m c e) -> p m u c e", m=4, u=2, e=2)[:, (j % 8) // 2]
                k_b = st["kT%d" % h][:].bitcast(BF16).rearrange("p (b u c e) -> p u b c e", b=16, u=2, e=2)
            else:
                q_b = st["qT%d" % m][:].bitcast(BF16).rearrange("p (a u c e) -> p a u c e", a=2, u=2, e=2)[:, al]
                k_b = st["kT%d" % h][:].bitcast(BF16).rearrange("p (u c e) -> p u c e", u=2, e=2)
            for n in range(4):
                u, e = n // 2, n % 2
                rhs = k_b[:, u, :, :, e] if h in V_HEADS else k_b[:, u, :, e]
                nc.tensor.matmul(s_t[:], lhsT=q_b[:, u, :, e], rhs=rhs, start=(n == 0), stop=(n == 3))
                if n < 3:
                    for go, fin in flat[begs[n]:ends[n]]:
                        go()
                        if fin is not None:
                            fin()

        def softmax_max(j):
            st["mx"] = small.tile([P, 1], F32, name="mx")
            nc.vector.tensor_reduce(out=st["mx"][:], in_=st["s%d" % j][:], axis=AX.X, op=ALU.max)

        def softmax_bias(j):
            nb = small.tile([P, 1], F32, name="nb")
            nc.vector.tensor_scalar(out=nb[:], in0=st["mx"][:], scalar1=-SCALE, scalar2=None, op0=ALU.mult)
            st["nb%d" % j] = nb

        def softmax_exp(j):
            e_t = ep.tile([P, SK], BF16, name="e")
            rs = eq.tile([P, 1], F32, name="rs")
            nc.scalar.activation(out=e_t[:], in_=st["s%d" % j][:], func=ACT.Exp, bias=st["nb%d" % j][:],
                                 scale=SCALE, accum_out=rs[:])
            st["e%d" % j] = e_t
            st["rs%d" % j] = rs

        def recip(j):
            ri = eq.tile([P, 1], F32, name="ri")
            nc.vector.reciprocal(out=ri[:], in_=st["rs%d" % j][:])
            st["ri%d" % j] = ri

        def stage1(ot):
            wc, ws = st["wc%d" % ot]
            acc = ps_a.tile([P, 4, P], F32, name="acc")
            for t in range(NXT):
                for g in range(4):
                    nc.tensor.matmul_mx(out=acc[:, t, :], lhsT=xc[:, t, g, :].bitcast(FP8X4), lhsT_scale=xs[:, t, g, :],
                                        rhs=wc[:, P * g:P * g + P].bitcast(FP8X4), rhs_scale=ws[:, P * g:P * g + P],
                                        start=(g == 0), stop=(g == 3))
            ig = grp.tile([P, P, 4], BF16, align_bytes=64, name="ig")
            nc.vector.tensor_tensor(out=ig[:], in0=acc[:].rearrange("p t o -> p o t"),
                                    in1=bias[:, P * ot:P * ot + P].unsqueeze(2).to_broadcast([P, P, 4]), op=ALU.add)
            st["ig%d" % ot] = ig

        def quant_imf(ot):
            h, a = ot // 4, ot % 4
            nc.vector.quantize_mx(out=imf_c[h][:, P * a:P * a + P].bitcast(FP8X4), scales=imf_s[h][:, P * a:P * a + P],
                                  in_=st["ig%d" % ot][:].rearrange("p o t -> p (o t)"))

        def pv(j, bank=None, on_vector=False, store_alone=False):
            h, a = j // 8, j % 8
            ec, es = st["ec%d" % j]
            pool, tag = bank or (ps_p, "pv")
            pv_t = pool.tile([P, DK], F32, name=tag)
            nc.tensor.matmul_mx(out=pv_t[:], lhsT=ec[:].bitcast(FP8X4), lhsT_scale=es[:], rhs=imf_c[h][:].bitcast(FP8X4),
                                rhs_scale=imf_s[h][:], start=True, stop=True)
            if a % 2 == 0:
                st["o"] = op.tile([P, 2, DK], F32, name="o_sb")
            if on_vector:
                nc.vector.tensor_scalar(out=st["o"][:, a % 2, :], in0=pv_t[:], scalar1=st["ri%d" % j][:], scalar2=None, op0=ALU.mult)
            else:
                nc.scalar.activation(out=st["o"][:, a % 2, :], in_=pv_t[:], func=ACT.Copy, scale=st["ri%d" % j][:])
            o_pair = o_b[h][a // 2] if h in V_HEADS else o_t[h][:, a - a % 2:a - a % 2 + 2, :]
            if store_alone:
                nc.sync.dma_start(out=o_pair[:, a % 2, :], in_=st["o"][:, a % 2, :])
            elif a % 2 == 1:
                nc.sync.dma_start(out=o_pair, in_=st["o"][:])

        run_jobs([k_job(0, 0), k_job(0, 1), first_q_job(0), first_q_job(1)])
        turns = [lambda: q_turn(3, 0, 0), lambda: q_turn(3, 0, 1), lambda: q_turn(3, 1, 0), lambda: q_turn(3, 1, 1),
                 lambda: k_turn(3, 0), lambda: k_turn(3, 1)]
        next_pv = 0
        owed = None
        i = 0
        while i < NQT:
            s1_now = 0 <= i - U_START - NXT - S1_LAG < NOT
            if i >= LATE_FROM:
                for dst, src in late[2 * (i - LATE_FROM):2 * (i - LATE_FROM) + 2]:
                    nc.sync.dma_start(out=dst, in_=src)
            jobs = []
            v = i - U_START
            if 0 <= v < NUNIT:
                jobs.append(u_job(v, 0))
            if owed is not None:
                jobs.append(([lambda j=owed: softmax_exp(j)], lambda: None))
            if 0 <= i - E_LAG < NQT:
                jobs.append(e_job(i - E_LAG))
            if 0 <= v < NUNIT:
                jobs.append(u_job(v, 1))
            if i % 2 == 0 and i // 2 + 1 < NQT // 2 and (i + 2) // 8 not in V_HEADS:
                jobs.append(q_job(i // 2 + 1))
            if i % 8 in K_AT and i // 8 + 1 < H and i // 8 + 1 not in V_HEADS:
                jobs.insert(0, k_job(i // 8 + 1, K_AT.index(i % 8)))
            if i < NQT:
                qk_with_transposes(i, jobs)
            else:
                run_jobs(jobs)
            ot_done = i - U_START - NXT - S1_LAG - 1
            if 0 <= ot_done < NOT:
                quant_imf(ot_done)
            softmax_max(i)
            if i >= E_LAG:
                quant_e(i - E_LAG)
            softmax_bias(i)
            if i >= E_LAG:
                recip(i - E_LAG)
            if 0 <= v < NUNIT:
                quant_u(v)
            todo = []
            while len(todo) < PV_PER_BUNCH and next_pv <= i - E_LAG - PV_LAG and i >= U_START + NXT + 4 * (next_pv // 8) + 3 + S1_LAG + 1:
                todo.append(next_pv)
                next_pv += 1
            if todo:
                pv(todo[0], store_alone=(i == NQT - 1))
            if s1_now or i == NQT - 1:
                softmax_exp(i)
                owed = None
            else:
                owed = i
            ot = i - U_START - NXT - S1_LAG
            if 0 <= ot < NOT:
                stage1(ot)
            for j in todo[1:]:
                pv(j)
            if 0 <= i - VEC_FROM < len(turns):
                turns[i - VEC_FROM]()
            i += 1
        n_last = NQT - 1
        run_jobs([e_job(n_last - 1)])
        quant_e(n_last - 1)
        recip(n_last - 1)
        for j in range(next_pv, n_last - 1):
            pv(j, bank=(ps_t, "tw"), store_alone=True)
        run_jobs([e_job(n_last)])
        quant_e(n_last)
        recip(n_last)
        pv(n_last - 1, bank=(ps_a, "acc"), store_alone=True)
        ec, es = st["ec%d" % n_last]
        for half in range(2):
            cols = slice(256 * half, 256 * half + 256)
            half_t = ps_s.tile([P, 256], F32, name="s")
            nc.tensor.matmul_mx(out=half_t[:], lhsT=ec[:].bitcast(FP8X4), lhsT_scale=es[:], rhs=imf_c[H - 1][:, cols].bitcast(FP8X4),
                                rhs_scale=imf_s[H - 1][:, cols], start=True, stop=True)
            dst = st["o"][:, 1, cols]
            if half == 0:
                nc.vector.tensor_scalar(out=dst, in0=half_t[:], scalar1=st["ri%d" % n_last][:], scalar2=None, op0=ALU.mult)
            else:
                nc.scalar.activation(out=dst, in_=half_t[:], func=ACT.Copy, scale=st["ri%d" % n_last][:])
            nc.sync.dma_start(out=o_b[H - 1][8 // 2 - 1][:, 1, cols], in_=dst)
